import numpy as np
import ml_dtypes


def mxq(x, axis, fmt="e4m3"):
    dtype, down = {"e4m3": (ml_dtypes.float8_e4m3fn, 7), "e5m2": (ml_dtypes.float8_e5m2, 14)}[fmt]
    v = np.moveaxis(np.asarray(x, np.float32).astype(ml_dtypes.bfloat16).astype(np.float64), axis, -1)
    blocks = v.reshape(v.shape[:-1] + (-1, 32))
    amax = np.abs(blocks).max(-1, keepdims=True)
    byte = np.maximum(np.where(amax > 0, np.frexp(amax)[1] - 1 + 127, 0) - down, 1)
    scale = np.exp2(byte - 127.0)
    codes = (blocks / scale).astype(np.float32).astype(dtype).astype(np.float64)
    return np.moveaxis((codes * scale).reshape(v.shape), -1, axis)


WIDE = False


def mx_kscale(k):
    if not WIDE:
        return np.ones(k)
    levels = np.array([10, -10, 5, -5, 0])
    a = np.random.permutation(np.resize(levels, k // 512 * 4)).reshape(k // 512, 4)
    idx = np.arange(k)
    return np.exp2(a[idx // 512, idx % 128 // 32])


BF16 = ml_dtypes.bfloat16


def bf(x):
    return np.asarray(x, np.float32).astype(BF16)


def f64(x):
    return np.asarray(x).astype(np.float64)


E2M1 = np.array([0.0, 0.5, 1.0, 1.5, 2.0, 3.0, 4.0, 6.0, -0.0, -0.5, -1.0, -1.5, -2.0, -3.0, -4.0, -6.0])


def pack_weight(w, fmt):
    k, n = w.shape
    w = f64(bf(w)).reshape(k // 32, 32, n)
    amax = np.abs(w).max(1)
    if fmt == "e4m3":
        byte = np.frexp(amax)[1] - 1 + 127 - 7
    else:
        mant, ex = np.frexp(amax / 6.0)
        byte = np.where(mant > 0.5, ex, ex - 1) + 127
    byte = np.clip(np.where(amax > 0, byte, 1), 1, 254)
    scaled = (w * np.exp2(127.0 - byte)[:, None, :]).reshape(k, n).astype(np.float32)
    by_word = np.ascontiguousarray(scaled.reshape(k // 512, 128, 4, n).transpose(0, 1, 3, 2))
    if fmt == "e4m3":
        words = by_word.astype(ml_dtypes.float8_e4m3fn).view(np.uint8)
    else:
        c = by_word.astype(ml_dtypes.float4_e2m1fn).view(np.uint8) & 0xF
        words = c[..., 0::2] | (c[..., 1::2] << 4)
    return np.ascontiguousarray(words), np.ascontiguousarray(byte.astype(np.uint8).reshape(k // 512, 16, n))


def unpack_weight(words, scales, fmt):
    g, p, n, _ = words.shape
    if fmt == "e4m3":
        vals = np.ascontiguousarray(words).view(ml_dtypes.float8_e4m3fn).astype(np.float64)
    else:
        nib = np.empty((g, p, n, 4), np.uint8)
        nib[..., 0::2] = words & 0xF
        nib[..., 1::2] = words >> 4
        vals = E2M1[nib]
    vals = vals * np.repeat(np.exp2(scales.astype(np.float64) - 127.0), 8, axis=1)[..., None]
    return vals.transpose(0, 1, 3, 2).reshape(g * 512, n)

def pack4(w):
    words, scales = pack_weight(w, "e2m1")
    return words.reshape(words.shape[0], 128, -1), scales


def unpack4(words, scales):
    return unpack_weight(words.reshape(words.shape[0], 128, -1, 2), scales, "e2m1")


B, S, E, H, DH, L = 2, 64, 16384, 16, 128, 512
NOPE = DH // 4
ROPE_D = DH - NOPE
THETA = 10000.0


def rope_tables(seq_len):
    freqs = 1.0 / THETA ** (np.arange(0, ROPE_D, 2) / ROPE_D)
    emb = np.arange(seq_len)[:, None] * freqs[None, :]
    return np.cos(emb), np.sin(emb)


def apply_rope(x, cos, sin):
    xe, xo = x[..., ::2], x[..., 1::2]
    return np.concatenate([xe * cos - xo * sin, xo * cos + xe * sin], axis=-1)


def setup_inputs():
    s = mx_kscale(E)
    x = bf(np.random.standard_normal((B, S, E)) * s)
    words, scales = pack4(np.random.standard_normal((E, H * DH)) / np.sqrt(E) / s[:, None])
    return {"x": x, "Wq_words": words, "Wq_scales": scales}


def reference(x, Wq_words, Wq_scales):
    q = (mxq(f64(x), 2, "e4m3") @ unpack4(Wq_words, Wq_scales)).reshape(B, S, H, DH).transpose(0, 2, 1, 3)
    q_nope, q_rope = q[..., :NOPE], q[..., NOPE:]
    cos, sin = rope_tables(S)
    q_rope = apply_rope(q_rope, cos, sin)
    return np.concatenate([q_nope, q_rope], axis=-1)

@@ -1,0 +1,210 @@
+import math
+from contextlib import ExitStack
+
+import concourse.masks as masks
+import concourse.mybir as mybir
+
+F32 = mybir.dt.float32
+BF16 = mybir.dt.bfloat16
+I32 = mybir.dt.int32
+U32 = mybir.dt.uint32
+U8 = mybir.dt.uint8
+FP8X4 = mybir.dt.float8_e4m3fn_x4
+FP4X4 = mybir.dt.float4_e2m1fn_x4
+ALU = mybir.AluOpType
+ACT = mybir.ActivationFunctionType
+
+B, S, E, H, DH = 2, 64, 16384, 16, 128
+N = H * DH
+NOPE = DH // 4
+HALF = (DH - NOPE) // 2
+THETA = 10000.0
+
+P = 128
+PACK = 4
+K_PASS = P * PACK
+PASSES = E // K_PASS
+BANK_COLS = 512
+BANKS = N // BANK_COLS
+BANK_HEADS = BANK_COLS // DH
+
+GROUP_PASSES = 8
+GROUPS = PASSES // GROUP_PASSES
+GROUP_K = GROUP_PASSES * K_PASS
+SCALE_DMA_PASSES = 4
+WORD_BUFS = 12
+
+TWO_PI_PARTS = (6.28125, 0.0019354820251464844, 2.0 * math.pi - 6.28125 - 0.0019354820251464844)
+ROUND_MAGIC = 12582912.0
+
+FLOPS = 2 * B * S * E * N
+
+
+def build_rotation_tables(nc, pool):
+    position_int = pool.tile([P, 1], I32)
+    nc.gpsimd.iota(position_int[:], pattern=[[0, 1]], base=0, channel_multiplier=1)
+    nc.vector.tensor_single_scalar(
+        out=position_int[:], in_=position_int[:], scalar=S - 1, op=ALU.bitwise_and
+    )
+    position = pool.tile([P, 1], F32)
+    nc.vector.tensor_copy(out=position[:], in_=position_int[:])
+
+    ratio = THETA ** (-1.0 / HALF)
+    frequency = pool.tile([P, HALF], F32)
+    nc.vector.memset(frequency[:, 0:1], 1.0)
+    filled = 1
+    while filled < HALF:
+        more = min(filled, HALF - filled)
+        nc.vector.tensor_single_scalar(
+            out=frequency[:, filled : filled + more],
+            in_=frequency[:, 0:more],
+            scalar=ratio**filled,
+            op=ALU.mult,
+        )
+        filled += more
+
+    angle = pool.tile([P, 2, HALF], F32)
+    nc.vector.tensor_scalar(
+        out=angle[:, 1, :], in0=frequency[:], scalar1=position[:, 0:1], scalar2=None, op0=ALU.mult
+    )
+    nc.vector.tensor_single_scalar(
+        out=angle[:, 0, :], in_=angle[:, 1, :], scalar=math.pi / 2.0, op=ALU.add
+    )
+
+    turns = pool.tile([P, 2, HALF], F32)
+    nc.vector.tensor_scalar(
+        out=turns[:],
+        in0=angle[:],
+        scalar1=1.0 / (2.0 * math.pi),
+        scalar2=ROUND_MAGIC,
+        op0=ALU.mult,
+        op1=ALU.add,
+    )
+    nc.vector.tensor_single_scalar(out=turns[:], in_=turns[:], scalar=ROUND_MAGIC, op=ALU.subtract)
+    for part in TWO_PI_PARTS:
+        nc.vector.scalar_tensor_tensor(
+            out=angle[:], in0=turns[:], scalar=-part, in1=angle[:], op0=ALU.mult, op1=ALU.add
+        )
+    cos_sin = pool.tile([P, 2, HALF], F32)
+    nc.scalar.activation(out=cos_sin[:], in_=angle[:], func=ACT.Sin)
+    return cos_sin
+
+
+def quantise_x_group(nc, flip_psum, stage, x_group, identity, codes, scales):
+    x_words = x_group[:].bitcast(F32)
+    pass_words = K_PASS // 2
+    grouped = stage.tile([P, GROUP_PASSES * P * PACK], BF16, align_bytes=64)
+    grouped_words = grouped[:].bitcast(F32).rearrange("p (l m u) -> p l m u", m=P, u=2)
+    for pair in range(GROUP_PASSES // 2):
+        flipped = flip_psum.tile([P, 2, 2, P], F32)
+        for l in range(2):
+            first = (2 * pair + l) * pass_words
+            for u in range(2):
+                nc.tensor.transpose(
+                    flipped[:, l, u, :], x_words[:, first + u : first + pass_words : 2], identity[:]
+                )
+        copy = nc.vector.tensor_copy if pair % 2 == 0 else nc.scalar.copy
+        copy(
+            out=grouped_words[:, 2 * pair : 2 * pair + 2, :, :],
+            in_=flipped[:].rearrange("p l u m -> p l m u"),
+        )
+    nc.vector.quantize_mx(out=codes[:].bitcast(FP8X4), scales=scales[:], in_=grouped[:])
+
+
+def load_scale_rows(nc, planes, Wq_scales, first_pass):
+    nc.vector.memset(planes[:].rearrange("p l n -> p (l n)").bitcast(I32), 0)
+    rows = Wq_scales.rearrange("g (half low) n -> low half g n", half=2)
+    for l in range(0, GROUP_PASSES, SCALE_DMA_PASSES):
+        for low in range(8):
+            partition = 32 * (low // 4) + low % 4
+            nc.sync.dma_start(
+                out=planes[partition:P:64, l : l + SCALE_DMA_PASSES, :].bitcast(I32),
+                in_=rows[low, :, first_pass + l : first_pass + l + SCALE_DMA_PASSES, :].bitcast(I32),
+            )
+
+
+def rotate_and_store(nc, out_pool, q_bank, cos_sin, out, bank):
+    q = q_bank[:].rearrange("p (h d) -> p h d", d=DH)
+    pairs = q[:, :, NOPE:].rearrange("p h (j e) -> p h e j", e=2)
+    table_shape = [P, BANK_HEADS, 2, HALF]
+    cos = cos_sin[:, 0:1, :].unsqueeze(1).to_broadcast(table_shape)
+    sin = cos_sin[:, 1:2, :].unsqueeze(1).to_broadcast(table_shape)
+
+    result = out_pool.tile([P, BANK_HEADS, DH], F32)
+    by_sin = out_pool.tile([P, BANK_HEADS, 2, HALF], F32)
+    first_half = result[:, :, NOPE : NOPE + HALF]
+    second_half = result[:, :, NOPE + HALF :]
+    nc.scalar.copy(out=result[:, :, :NOPE], in_=q[:, :, :NOPE])
+    nc.vector.tensor_tensor(
+        out=result[:, :, NOPE:].rearrange("p h (e j) -> p h e j", e=2), in0=pairs, in1=cos, op=ALU.mult
+    )
+    nc.vector.tensor_tensor(out=by_sin[:], in0=pairs, in1=sin, op=ALU.mult)
+    nc.vector.tensor_tensor(out=first_half, in0=first_half, in1=by_sin[:, :, 1, :], op=ALU.subtract)
+    nc.vector.tensor_tensor(out=second_half, in0=second_half, in1=by_sin[:, :, 0, :], op=ALU.add)
+
+    heads = slice(bank * BANK_HEADS, (bank + 1) * BANK_HEADS)
+    for b in range(B):
+        nc.sync.dma_start(
+            out=out[b, heads, :, :].rearrange("h s d -> s h d"), in_=result[b * S : (b + 1) * S, :, :]
+        )
+
+
+def tile_mla_pb_k_kernel(tc, x, Wq_words, Wq_scales, out):
+    nc = tc.nc
+    x_rows = x.rearrange("b s e -> (b s) e")
+    with ExitStack() as ctx:
+        consts = ctx.enter_context(tc.tile_pool(name="consts", bufs=1))
+        x_pool = ctx.enter_context(tc.tile_pool(name="x_pool", bufs=GROUPS))
+        stage = ctx.enter_context(tc.tile_pool(name="stage", bufs=2))
+        keep = ctx.enter_context(tc.tile_pool(name="keep", bufs=1))
+        word_pool = ctx.enter_context(tc.tile_pool(name="word_pool", bufs=WORD_BUFS))
+        out_pool = ctx.enter_context(tc.tile_pool(name="out_pool", bufs=BANKS))
+        flip_psum = ctx.enter_context(tc.psum_pool(name="flip_psum", bufs=8 - BANKS))
+        q_psum = ctx.enter_context(tc.psum_pool(name="q_psum", bufs=1))
+
+        x_groups = []
+        for group in range(GROUPS):
+            x_group = x_pool.tile([P, GROUP_K], BF16)
+            nc.sync.dma_start(out=x_group[:], in_=x_rows[:, group * GROUP_K : (group + 1) * GROUP_K])
+            x_groups.append(x_group)
+
+        identity = consts.tile([P, P], F32)
+        masks.make_identity(nc, identity[:])
+        cos_sin = build_rotation_tables(nc, consts)
+
+        x_codes = []
+        x_scales = []
+        for group in range(GROUPS):
+            codes = keep.tile([P, GROUP_PASSES * P], U32, name="x_codes%d" % group, align_bytes=64)
+            scales = keep.tile([P, GROUP_PASSES * P], U8, name="x_scales%d" % group, align_bytes=64)
+            quantise_x_group(nc, flip_psum, stage, x_groups[group], identity, codes, scales)
+            x_codes.append(codes)
+            x_scales.append(scales)
+
+        q_banks = []
+        for bank in range(BANKS):
+            q_bank = q_psum.tile([P, BANK_COLS], F32, name="q_bank%d" % bank)
+            q_banks.append(q_bank)
+
+        for group in range(GROUPS):
+            first_pass = group * GROUP_PASSES
+            planes = keep.tile([P, GROUP_PASSES, N], U8, name="w_planes%d" % group, align_bytes=64)
+            load_scale_rows(nc, planes, Wq_scales, first_pass)
+            for l in range(GROUP_PASSES):
+                g = first_pass + l
+                words = word_pool.tile([P, 2 * N], U8, align_bytes=64)
+                nc.sync.dma_start(out=words[:].bitcast(I32), in_=Wq_words[g].bitcast(I32))
+                tokens = slice(l * P, (l + 1) * P)
+                for bank in range(BANKS):
+                    nc.tensor.matmul_mx(
+                        out=q_banks[bank][:],
+                        lhsT=x_codes[group][:, tokens].bitcast(FP8X4),
+                        lhsT_scale=x_scales[group][:, tokens],
+                        rhs=words[:, 2 * bank * BANK_COLS : 2 * (bank + 1) * BANK_COLS].bitcast(FP4X4),
+                        rhs_scale=planes[:, l, bank * BANK_COLS : (bank + 1) * BANK_COLS],
+                        start=(g == 0),
+                        stop=(g == PASSES - 1),
+                    )
+
+        for bank in range(BANKS):
+            rotate_and_store(nc, out_pool, q_banks[bank], cos_sin, out, bank)

@@ -33,6 +33,7 @@ GROUPS = PASSES // GROUP_PASSES
 GROUP_K = GROUP_PASSES * K_PASS
 SCALE_DMA_PASSES = 4
 WORD_BUFS = 12
+END_PASSES = 4
 
 TWO_PI_PARTS = (6.28125, 0.0019354820251464844, 2.0 * math.pi - 6.28125 - 0.0019354820251464844)
 ROUND_MAGIC = 12582912.0
@@ -186,25 +187,45 @@ def tile_mla_pb_k_kernel(tc, x, Wq_words, Wq_scales, out):
             q_bank = q_psum.tile([P, BANK_COLS], F32, name="q_bank%d" % bank)
             q_banks.append(q_bank)
 
-        for group in range(GROUPS):
-            first_pass = group * GROUP_PASSES
-            planes = keep.tile([P, GROUP_PASSES, N], U8, name="w_planes%d" % group, align_bytes=64)
-            load_scale_rows(nc, planes, Wq_scales, first_pass)
-            for l in range(GROUP_PASSES):
-                g = first_pass + l
-                words = word_pool.tile([P, 2 * N], U8, align_bytes=64)
-                nc.sync.dma_start(out=words[:].bitcast(I32), in_=Wq_words[g].bitcast(I32))
-                tokens = slice(l * P, (l + 1) * P)
-                for bank in range(BANKS):
-                    nc.tensor.matmul_mx(
-                        out=q_banks[bank][:],
-                        lhsT=x_codes[group][:, tokens].bitcast(FP8X4),
-                        lhsT_scale=x_scales[group][:, tokens],
-                        rhs=words[:, 2 * bank * BANK_COLS : 2 * (bank + 1) * BANK_COLS].bitcast(FP4X4),
-                        rhs_scale=planes[:, l, bank * BANK_COLS : (bank + 1) * BANK_COLS],
-                        start=(g == 0),
-                        stop=(g == PASSES - 1),
-                    )
+        w_planes = []
 
+        def mx_pass(g, bank, bank_words):
+            group, local = divmod(g, GROUP_PASSES)
+            tokens = slice(local * P, (local + 1) * P)
+            nc.tensor.matmul_mx(
+                out=q_banks[bank][:],
+                lhsT=x_codes[group][:, tokens].bitcast(FP8X4),
+                lhsT_scale=x_scales[group][:, tokens],
+                rhs=bank_words.bitcast(FP4X4),
+                rhs_scale=w_planes[group][:, local, bank * BANK_COLS : (bank + 1) * BANK_COLS],
+                start=(g == 0),
+                stop=(g == PASSES - 1),
+            )
+
+        bank_bytes = 2 * BANK_COLS
+        for g in range(PASSES - END_PASSES):
+            if g % GROUP_PASSES == 0:
+                planes = keep.tile(
+                    [P, GROUP_PASSES, N], U8, name="w_planes%d" % (g // GROUP_PASSES), align_bytes=64
+                )
+                load_scale_rows(nc, planes, Wq_scales, g)
+                w_planes.append(planes)
+            words = word_pool.tile([P, BANKS * bank_bytes], U8, align_bytes=64)
+            nc.sync.dma_start(out=words[:].bitcast(I32), in_=Wq_words[g].bitcast(I32))
+            for bank in range(BANKS):
+                mx_pass(g, bank, words[:, bank * bank_bytes : (bank + 1) * bank_bytes])
+
+        end_words = []
         for bank in range(BANKS):
+            words = word_pool.tile([P, END_PASSES, bank_bytes], U8, align_bytes=64)
+            nc.sync.dma_start(
+                out=words[:].bitcast(I32),
+                in_=Wq_words[PASSES - END_PASSES :, :, bank * bank_bytes : (bank + 1) * bank_bytes]
+                .rearrange("g p c -> p g c")
+                .bitcast(I32),
+            )
+            end_words.append(words)
+        for bank in range(BANKS):
+            for i in range(END_PASSES):
+                mx_pass(PASSES - END_PASSES + i, bank, end_words[bank][:, i, :])
             rotate_and_store(nc, out_pool, q_banks[bank], cos_sin, out, bank)

@@ -31,7 +31,6 @@ BANK_HEADS = BANK_COLS // DH
 GROUP_PASSES = 8
 GROUPS = PASSES // GROUP_PASSES
 GROUP_K = GROUP_PASSES * K_PASS
-SCALE_DMA_PASSES = 4
 WORD_BUFS = 12
 END_PASSES = 4
 
@@ -112,15 +111,16 @@ def quantise_x_group(nc, flip_psum, stage, x_group, identity, codes, scales):
     nc.vector.quantize_mx(out=codes[:].bitcast(FP8X4), scales=scales[:], in_=grouped[:])
 
 
-def load_scale_rows(nc, planes, Wq_scales, first_pass):
-    nc.vector.memset(planes[:].rearrange("p l n -> p (l n)").bitcast(I32), 0)
-    rows = Wq_scales.rearrange("g (half low) n -> low half g n", half=2)
-    for l in range(0, GROUP_PASSES, SCALE_DMA_PASSES):
-        for low in range(8):
-            partition = 32 * (low // 4) + low % 4
+def load_scale_rows(nc, planes, Wq_scales):
+    for first in range(0, PASSES, GROUP_PASSES):
+        nc.vector.memset(planes[:, first : first + GROUP_PASSES, :].rearrange("p l n -> p (l n)").bitcast(I32), 0)
+    rows = Wq_scales.rearrange("g (q one) n -> q one g n", one=1)
+    for low in range(4):
+        for quadrant in (0, 2, 1, 3):
+            partition = 32 * quadrant + low
             nc.sync.dma_start(
-                out=planes[partition:P:64, l : l + SCALE_DMA_PASSES, :].bitcast(I32),
-                in_=rows[low, :, first_pass + l : first_pass + l + SCALE_DMA_PASSES, :].bitcast(I32),
+                out=planes[partition : partition + 1, :, :].bitcast(I32),
+                in_=rows[4 * quadrant + low].bitcast(I32),
             )
 
 
@@ -187,7 +187,8 @@ def tile_mla_pb_k_kernel(tc, x, Wq_words, Wq_scales, out):
             q_bank = q_psum.tile([P, BANK_COLS], F32, name="q_bank%d" % bank)
             q_banks.append(q_bank)
 
-        w_planes = []
+        w_planes = keep.tile([P, PASSES, N], U8, name="w_planes", align_bytes=64)
+        load_scale_rows(nc, w_planes, Wq_scales)
 
         def mx_pass(g, bank, bank_words):
             group, local = divmod(g, GROUP_PASSES)
@@ -197,19 +198,13 @@ def tile_mla_pb_k_kernel(tc, x, Wq_words, Wq_scales, out):
                 lhsT=x_codes[group][:, tokens].bitcast(FP8X4),
                 lhsT_scale=x_scales[group][:, tokens],
                 rhs=bank_words.bitcast(FP4X4),
-                rhs_scale=w_planes[group][:, local, bank * BANK_COLS : (bank + 1) * BANK_COLS],
+                rhs_scale=w_planes[:, g, bank * BANK_COLS : (bank + 1) * BANK_COLS],
                 start=(g == 0),
                 stop=(g == PASSES - 1),
             )
 
         bank_bytes = 2 * BANK_COLS
         for g in range(PASSES - END_PASSES):
-            if g % GROUP_PASSES == 0:
-                planes = keep.tile(
-                    [P, GROUP_PASSES, N], U8, name="w_planes%d" % (g // GROUP_PASSES), align_bytes=64
-                )
-                load_scale_rows(nc, planes, Wq_scales, g)
-                w_planes.append(planes)
             words = word_pool.tile([P, BANKS * bank_bytes], U8, align_bytes=64)
             nc.sync.dma_start(out=words[:].bitcast(I32), in_=Wq_words[g].bitcast(I32))
             for bank in range(BANKS):

@@ -31,7 +31,7 @@ BANK_HEADS = BANK_COLS // DH
 GROUP_PASSES = 8
 GROUPS = PASSES // GROUP_PASSES
 GROUP_K = GROUP_PASSES * K_PASS
-WORD_BUFS = 12
+WORD_BUFS = 20
 END_PASSES = 4
 
 TWO_PI_PARTS = (6.28125, 0.0019354820251464844, 2.0 * math.pi - 6.28125 - 0.0019354820251464844)
@@ -112,8 +112,6 @@ def quantise_x_group(nc, flip_psum, stage, x_group, identity, codes, scales):
 
 
 def load_scale_rows(nc, planes, Wq_scales):
-    for first in range(0, PASSES, GROUP_PASSES):
-        nc.vector.memset(planes[:, first : first + GROUP_PASSES, :].rearrange("p l n -> p (l n)").bitcast(I32), 0)
     rows = Wq_scales.rearrange("g (q one) n -> q one g n", one=1)
     for low in range(4):
         for quadrant in (0, 2, 1, 3):
@@ -163,11 +161,17 @@ def tile_mla_pb_k_kernel(tc, x, Wq_words, Wq_scales, out):
         flip_psum = ctx.enter_context(tc.psum_pool(name="flip_psum", bufs=8 - BANKS))
         q_psum = ctx.enter_context(tc.psum_pool(name="q_psum", bufs=1))
 
+        ctx.enter_context(tc.manual_schedule(engines={mybir.EngineType.SP}))
+
+        w_planes = keep.tile([P, PASSES, N], U8, name="w_planes", align_bytes=64)
+        nc.vector.memset(w_planes[:].rearrange("p l n -> p (l n)").bitcast(I32), 0)
+
         x_groups = []
         for group in range(GROUPS):
             x_group = x_pool.tile([P, GROUP_K], BF16)
             nc.sync.dma_start(out=x_group[:], in_=x_rows[:, group * GROUP_K : (group + 1) * GROUP_K])
             x_groups.append(x_group)
+        load_scale_rows(nc, w_planes, Wq_scales)
 
         identity = consts.tile([P, P], F32)
         masks.make_identity(nc, identity[:])
@@ -186,9 +190,6 @@ def tile_mla_pb_k_kernel(tc, x, Wq_words, Wq_scales, out):
         for bank in range(BANKS):
             q_bank = q_psum.tile([P, BANK_COLS], F32, name="q_bank%d" % bank)
             q_banks.append(q_bank)
-
-        w_planes = keep.tile([P, PASSES, N], U8, name="w_planes", align_bytes=64)
-        load_scale_rows(nc, w_planes, Wq_scales)
 
         def mx_pass(g, bank, bank_words):
             group, local = divmod(g, GROUP_PASSES)

@@ -31,8 +31,10 @@ BANK_HEADS = BANK_COLS // DH
 GROUP_PASSES = 8
 GROUPS = PASSES // GROUP_PASSES
 GROUP_K = GROUP_PASSES * K_PASS
-WORD_BUFS = 20
-END_PASSES = 4
+SCALE_PASSES = 16
+WORD_BUFS = 12
+END_PASSES = 8
+LAST_PASSES = 2
 
 TWO_PI_PARTS = (6.28125, 0.0019354820251464844, 2.0 * math.pi - 6.28125 - 0.0019354820251464844)
 ROUND_MAGIC = 12582912.0
@@ -113,13 +115,15 @@ def quantise_x_group(nc, flip_psum, stage, x_group, identity, codes, scales):
 
 def load_scale_rows(nc, planes, Wq_scales):
     rows = Wq_scales.rearrange("g (q one) n -> q one g n", one=1)
-    for low in range(4):
-        for quadrant in (0, 2, 1, 3):
-            partition = 32 * quadrant + low
-            nc.sync.dma_start(
-                out=planes[partition : partition + 1, :, :].bitcast(I32),
-                in_=rows[4 * quadrant + low].bitcast(I32),
-            )
+    for first in range(0, PASSES, SCALE_PASSES):
+        passes = slice(first, first + SCALE_PASSES)
+        for low in range(4):
+            for quadrant in (0, 2, 1, 3):
+                partition = 32 * quadrant + low
+                nc.sync.dma_start(
+                    out=planes[partition : partition + 1, passes, :].bitcast(I32),
+                    in_=rows[4 * quadrant + low, :, passes, :].bitcast(I32),
+                )
 
 
 def rotate_and_store(nc, out_pool, q_bank, cos_sin, out, bank):
@@ -133,11 +137,11 @@ def rotate_and_store(nc, out_pool, q_bank, cos_sin, out, bank):
     by_sin = out_pool.tile([P, BANK_HEADS, 2, HALF], F32)
     first_half = result[:, :, NOPE : NOPE + HALF]
     second_half = result[:, :, NOPE + HALF :]
-    nc.scalar.copy(out=result[:, :, :NOPE], in_=q[:, :, :NOPE])
     nc.vector.tensor_tensor(
         out=result[:, :, NOPE:].rearrange("p h (e j) -> p h e j", e=2), in0=pairs, in1=cos, op=ALU.mult
     )
     nc.vector.tensor_tensor(out=by_sin[:], in0=pairs, in1=sin, op=ALU.mult)
+    nc.scalar.copy(out=result[:, :, :NOPE], in_=q[:, :, :NOPE])
     nc.vector.tensor_tensor(out=first_half, in0=first_half, in1=by_sin[:, :, 1, :], op=ALU.subtract)
     nc.vector.tensor_tensor(out=second_half, in0=second_half, in1=by_sin[:, :, 0, :], op=ALU.add)
 
@@ -157,6 +161,7 @@ def tile_mla_pb_k_kernel(tc, x, Wq_words, Wq_scales, out):
         stage = ctx.enter_context(tc.tile_pool(name="stage", bufs=2))
         keep = ctx.enter_context(tc.tile_pool(name="keep", bufs=1))
         word_pool = ctx.enter_context(tc.tile_pool(name="word_pool", bufs=WORD_BUFS))
+        end_pool = ctx.enter_context(tc.tile_pool(name="end_pool", bufs=1))
         out_pool = ctx.enter_context(tc.tile_pool(name="out_pool", bufs=BANKS))
         flip_psum = ctx.enter_context(tc.psum_pool(name="flip_psum", bufs=8 - BANKS))
         q_psum = ctx.enter_context(tc.psum_pool(name="q_psum", bufs=1))
@@ -211,17 +216,27 @@ def tile_mla_pb_k_kernel(tc, x, Wq_words, Wq_scales, out):
             for bank in range(BANKS):
                 mx_pass(g, bank, words[:, bank * bank_bytes : (bank + 1) * bank_bytes])
 
+        first_end = PASSES - END_PASSES
+        end_loads = []
+        end_loads.append((0, 2, first_end, END_PASSES // 2))
+        end_loads.append((0, 2, first_end + END_PASSES // 2, END_PASSES // 2))
+        end_loads.append((2, 1, first_end, END_PASSES))
+        end_loads.append((3, 1, first_end, END_PASSES - LAST_PASSES))
+        end_loads.append((3, 1, PASSES - LAST_PASSES, LAST_PASSES))
         end_words = []
-        for bank in range(BANKS):
-            words = word_pool.tile([P, END_PASSES, bank_bytes], U8, align_bytes=64)
+        for bank, banks, first, passes in end_loads:
+            words = end_pool.tile([P, passes, banks * bank_bytes], U8, name="end_words%d" % len(end_words), align_bytes=64)
             nc.sync.dma_start(
                 out=words[:].bitcast(I32),
-                in_=Wq_words[PASSES - END_PASSES :, :, bank * bank_bytes : (bank + 1) * bank_bytes]
+                in_=Wq_words[first : first + passes, :, bank * bank_bytes : (bank + banks) * bank_bytes]
                 .rearrange("g p c -> p g c")
                 .bitcast(I32),
             )
             end_words.append(words)
-        for bank in range(BANKS):
-            for i in range(END_PASSES):
-                mx_pass(PASSES - END_PASSES + i, bank, end_words[bank][:, i, :])
-            rotate_and_store(nc, out_pool, q_banks[bank], cos_sin, out, bank)
+        for (first_bank, banks, first, passes), words in zip(end_loads, end_words):
+            for bank in range(first_bank, first_bank + banks):
+                start = (bank - first_bank) * bank_bytes
+                for i in range(passes):
+                    mx_pass(first + i, bank, words[:, i, start : start + bank_bytes])
+                if first + passes == PASSES:
+                    rotate_and_store(nc, out_pool, q_banks[bank], cos_sin, out, bank)

@@ -31,8 +31,11 @@ BANK_HEADS = BANK_COLS // DH
 GROUP_PASSES = 8
 GROUPS = PASSES // GROUP_PASSES
 GROUP_K = GROUP_PASSES * K_PASS
-SCALE_PASSES = 16
-WORD_BUFS = 12
+SCALE_DMA_PASSES = (8, 8, 8, 4, 4)
+LOAD_PASSES = 2
+SINGLE_PASSES = 4
+WORD_BUFS = 6
+X_LOADS = 2
 END_PASSES = 8
 LAST_PASSES = 2
 
@@ -93,7 +96,7 @@ def build_rotation_tables(nc, pool):
 
 
 def quantise_x_group(nc, flip_psum, stage, x_group, identity, codes, scales):
-    x_words = x_group[:].bitcast(F32)
+    x_words = x_group.bitcast(F32)
     pass_words = K_PASS // 2
     grouped = stage.tile([P, GROUP_PASSES * P * PACK], BF16, align_bytes=64)
     grouped_words = grouped[:].bitcast(F32).rearrange("p (l m u) -> p l m u", m=P, u=2)
@@ -114,16 +117,16 @@ def quantise_x_group(nc, flip_psum, stage, x_group, identity, codes, scales):
 
 
 def load_scale_rows(nc, planes, Wq_scales):
-    rows = Wq_scales.rearrange("g (q one) n -> q one g n", one=1)
-    for first in range(0, PASSES, SCALE_PASSES):
-        passes = slice(first, first + SCALE_PASSES)
-        for low in range(4):
-            for quadrant in (0, 2, 1, 3):
-                partition = 32 * quadrant + low
-                nc.sync.dma_start(
-                    out=planes[partition : partition + 1, passes, :].bitcast(I32),
-                    in_=rows[4 * quadrant + low, :, passes, :].bitcast(I32),
-                )
+    rows = Wq_scales.rearrange("g (half low) n -> low half g n", half=2)
+    first = 0
+    for count in SCALE_DMA_PASSES:
+        for low in range(8):
+            partition = 32 * (low // 4) + low % 4
+            nc.sync.dma_start(
+                out=planes[partition:P:64, first : first + count, :].bitcast(I32),
+                in_=rows[low, :, first : first + count, :].bitcast(I32),
+            )
+        first += count
 
 
 def rotate_and_store(nc, out_pool, q_bank, cos_sin, out, bank):
@@ -157,7 +160,7 @@ def tile_mla_pb_k_kernel(tc, x, Wq_words, Wq_scales, out):
     x_rows = x.rearrange("b s e -> (b s) e")
     with ExitStack() as ctx:
         consts = ctx.enter_context(tc.tile_pool(name="consts", bufs=1))
-        x_pool = ctx.enter_context(tc.tile_pool(name="x_pool", bufs=GROUPS))
+        x_pool = ctx.enter_context(tc.tile_pool(name="x_pool", bufs=X_LOADS))
         stage = ctx.enter_context(tc.tile_pool(name="stage", bufs=2))
         keep = ctx.enter_context(tc.tile_pool(name="keep", bufs=1))
         word_pool = ctx.enter_context(tc.tile_pool(name="word_pool", bufs=WORD_BUFS))
@@ -172,10 +175,12 @@ def tile_mla_pb_k_kernel(tc, x, Wq_words, Wq_scales, out):
         nc.vector.memset(w_planes[:].rearrange("p l n -> p (l n)").bitcast(I32), 0)
 
         x_groups = []
-        for group in range(GROUPS):
-            x_group = x_pool.tile([P, GROUP_K], BF16)
-            nc.sync.dma_start(out=x_group[:], in_=x_rows[:, group * GROUP_K : (group + 1) * GROUP_K])
-            x_groups.append(x_group)
+        load_k = E // X_LOADS
+        for load in range(X_LOADS):
+            x_part = x_pool.tile([P, load_k], BF16)
+            nc.sync.dma_start(out=x_part[:], in_=x_rows[:, load * load_k : (load + 1) * load_k])
+            for first in range(0, load_k, GROUP_K):
+                x_groups.append(x_part[:, first : first + GROUP_K])
         load_scale_rows(nc, w_planes, Wq_scales)
 
         identity = consts.tile([P, P], F32)
@@ -210,11 +215,17 @@ def tile_mla_pb_k_kernel(tc, x, Wq_words, Wq_scales, out):
             )
 
         bank_bytes = 2 * BANK_COLS
-        for g in range(PASSES - END_PASSES):
-            words = word_pool.tile([P, BANKS * bank_bytes], U8, align_bytes=64)
-            nc.sync.dma_start(out=words[:].bitcast(I32), in_=Wq_words[g].bitcast(I32))
-            for bank in range(BANKS):
-                mx_pass(g, bank, words[:, bank * bank_bytes : (bank + 1) * bank_bytes])
+        g = 0
+        while g < PASSES - END_PASSES:
+            passes = LOAD_PASSES if g < PASSES - END_PASSES - SINGLE_PASSES else 1
+            words = word_pool.tile([P, passes, BANKS * bank_bytes], U8, align_bytes=64)
+            nc.sync.dma_start(
+                out=words[:].bitcast(I32), in_=Wq_words[g : g + passes].rearrange("g p c -> p g c").bitcast(I32)
+            )
+            for i in range(passes):
+                for bank in range(BANKS):
+                    mx_pass(g + i, bank, words[:, i, bank * bank_bytes : (bank + 1) * bank_bytes])
+            g += passes
 
         first_end = PASSES - END_PASSES
         end_loads = []

@@ -98,7 +98,7 @@ def build_rotation_tables(nc, pool):
 def quantise_x_group(nc, flip_psum, stage, x_group, identity, codes, scales):
     x_words = x_group.bitcast(F32)
     pass_words = K_PASS // 2
-    grouped = stage.tile([P, GROUP_PASSES * P * PACK], BF16, align_bytes=64)
+    grouped = stage.tile([P, GROUP_PASSES * P * PACK], BF16, align_bytes=256)
     grouped_words = grouped[:].bitcast(F32).rearrange("p (l m u) -> p l m u", m=P, u=2)
     for pair in range(GROUP_PASSES // 2):
         flipped = flip_psum.tile([P, 2, 2, P], F32)
@@ -171,7 +171,7 @@ def tile_mla_pb_k_kernel(tc, x, Wq_words, Wq_scales, out):
 
         ctx.enter_context(tc.manual_schedule(engines={mybir.EngineType.SP}))
 
-        w_planes = keep.tile([P, PASSES, N], U8, name="w_planes", align_bytes=64)
+        w_planes = keep.tile([P, PASSES, N], U8, name="w_planes", align_bytes=256)
         nc.vector.memset(w_planes[:].rearrange("p l n -> p (l n)").bitcast(I32), 0)
 
         x_groups = []
@@ -190,8 +190,8 @@ def tile_mla_pb_k_kernel(tc, x, Wq_words, Wq_scales, out):
         x_codes = []
         x_scales = []
         for group in range(GROUPS):
-            codes = keep.tile([P, GROUP_PASSES * P], U32, name="x_codes%d" % group, align_bytes=64)
-            scales = keep.tile([P, GROUP_PASSES * P], U8, name="x_scales%d" % group, align_bytes=64)
+            codes = keep.tile([P, GROUP_PASSES * P], U32, name="x_codes%d" % group, align_bytes=256)
+            scales = keep.tile([P, GROUP_PASSES * P], U8, name="x_scales%d" % group, align_bytes=256)
             quantise_x_group(nc, flip_psum, stage, x_groups[group], identity, codes, scales)
             x_codes.append(codes)
             x_scales.append(scales)
@@ -217,8 +217,8 @@ def tile_mla_pb_k_kernel(tc, x, Wq_words, Wq_scales, out):
         bank_bytes = 2 * BANK_COLS
         g = 0
         while g < PASSES - END_PASSES:
-            passes = LOAD_PASSES if g < PASSES - END_PASSES - SINGLE_PASSES else 1
-            words = word_pool.tile([P, passes, BANKS * bank_bytes], U8, align_bytes=64)
+            passes = LOAD_PASSES if SINGLE_PASSES <= g < PASSES - END_PASSES - SINGLE_PASSES else 1
+            words = word_pool.tile([P, passes, BANKS * bank_bytes], U8, align_bytes=256)
             nc.sync.dma_start(
                 out=words[:].bitcast(I32), in_=Wq_words[g : g + passes].rearrange("g p c -> p g c").bitcast(I32)
             )
@@ -236,7 +236,7 @@ def tile_mla_pb_k_kernel(tc, x, Wq_words, Wq_scales, out):
         end_loads.append((3, 1, PASSES - LAST_PASSES, LAST_PASSES))
         end_words = []
         for bank, banks, first, passes in end_loads:
-            words = end_pool.tile([P, passes, banks * bank_bytes], U8, name="end_words%d" % len(end_words), align_bytes=64)
+            words = end_pool.tile([P, passes, banks * bank_bytes], U8, name="end_words%d" % len(end_words), align_bytes=256)
             nc.sync.dma_start(
                 out=words[:].bitcast(I32),
                 in_=Wq_words[first : first + passes, :, bank * bank_bytes : (bank + banks) * bank_bytes]

@@ -31,6 +31,7 @@ BANK_HEADS = BANK_COLS // DH
 GROUP_PASSES = 8
 GROUPS = PASSES // GROUP_PASSES
 GROUP_K = GROUP_PASSES * K_PASS
+PLANE_PASSES = 8
 SCALE_DMA_PASSES = (8, 8, 8, 4, 4)
 LOAD_PASSES = 2
 SINGLE_PASSES = 4
@@ -123,7 +124,9 @@ def load_scale_rows(nc, planes, Wq_scales):
         for low in range(8):
             partition = 32 * (low // 4) + low % 4
             nc.sync.dma_start(
-                out=planes[partition:P:64, first : first + count, :].bitcast(I32),
+                out=planes[first // PLANE_PASSES][
+                    partition:P:64, first % PLANE_PASSES : first % PLANE_PASSES + count, :
+                ].bitcast(I32),
                 in_=rows[low, :, first : first + count, :].bitcast(I32),
             )
         first += count
@@ -171,8 +174,11 @@ def tile_mla_pb_k_kernel(tc, x, Wq_words, Wq_scales, out):
 
         ctx.enter_context(tc.manual_schedule(engines={mybir.EngineType.SP}))
 
-        w_planes = keep.tile([P, PASSES, N], U8, name="w_planes", align_bytes=256)
-        nc.vector.memset(w_planes[:].rearrange("p l n -> p (l n)").bitcast(I32), 0)
+        w_planes = []
+        for i in range(PASSES // PLANE_PASSES):
+            plane = keep.tile([P, PLANE_PASSES, N], U8, name="w_planes%d" % i, align_bytes=256)
+            nc.vector.memset(plane[:].rearrange("p l n -> p (l n)").bitcast(I32), 0)
+            w_planes.append(plane)
 
         x_groups = []
         load_k = E // X_LOADS
@@ -209,7 +215,9 @@ def tile_mla_pb_k_kernel(tc, x, Wq_words, Wq_scales, out):
                 lhsT=x_codes[group][:, tokens].bitcast(FP8X4),
                 lhsT_scale=x_scales[group][:, tokens],
                 rhs=bank_words.bitcast(FP4X4),
-                rhs_scale=w_planes[:, g, bank * BANK_COLS : (bank + 1) * BANK_COLS],
+                rhs_scale=w_planes[g // PLANE_PASSES][
+                    :, g % PLANE_PASSES, bank * BANK_COLS : (bank + 1) * BANK_COLS
+                ],
                 start=(g == 0),
                 stop=(g == PASSES - 1),
             )

@@ -31,8 +31,7 @@ BANK_HEADS = BANK_COLS // DH
 GROUP_PASSES = 8
 GROUPS = PASSES // GROUP_PASSES
 GROUP_K = GROUP_PASSES * K_PASS
-PLANE_PASSES = 8
-SCALE_DMA_PASSES = (8, 8, 8, 4, 4)
+SCALE_DMA_PASSES = (28, 4)
 LOAD_PASSES = 2
 SINGLE_PASSES = 4
 WORD_BUFS = 6
@@ -120,13 +119,11 @@ def quantise_x_group(nc, flip_psum, stage, x_group, identity, codes, scales):
 def load_scale_rows(nc, planes, Wq_scales):
     rows = Wq_scales.rearrange("g (half low) n -> low half g n", half=2)
     first = 0
-    for count in SCALE_DMA_PASSES:
+    for plane, count in zip(planes, SCALE_DMA_PASSES):
         for low in range(8):
             partition = 32 * (low // 4) + low % 4
             nc.sync.dma_start(
-                out=planes[first // PLANE_PASSES][
-                    partition:P:64, first % PLANE_PASSES : first % PLANE_PASSES + count, :
-                ].bitcast(I32),
+                out=plane[partition:P:64, :, :].bitcast(I32),
                 in_=rows[low, :, first : first + count, :].bitcast(I32),
             )
         first += count
@@ -175,10 +172,13 @@ def tile_mla_pb_k_kernel(tc, x, Wq_words, Wq_scales, out):
         ctx.enter_context(tc.manual_schedule(engines={mybir.EngineType.SP}))
 
         w_planes = []
-        for i in range(PASSES // PLANE_PASSES):
-            plane = keep.tile([P, PLANE_PASSES, N], U8, name="w_planes%d" % i, align_bytes=256)
+        pass_planes = []
+        for count in SCALE_DMA_PASSES:
+            plane = keep.tile([P, count, N], U8, name="w_planes%d" % len(w_planes), align_bytes=256)
             nc.vector.memset(plane[:].rearrange("p l n -> p (l n)").bitcast(I32), 0)
             w_planes.append(plane)
+            for l in range(count):
+                pass_planes.append(plane[:, l, :])
 
         x_groups = []
         load_k = E // X_LOADS
@@ -215,9 +215,7 @@ def tile_mla_pb_k_kernel(tc, x, Wq_words, Wq_scales, out):
                 lhsT=x_codes[group][:, tokens].bitcast(FP8X4),
                 lhsT_scale=x_scales[group][:, tokens],
                 rhs=bank_words.bitcast(FP4X4),
-                rhs_scale=w_planes[g // PLANE_PASSES][
-                    :, g % PLANE_PASSES, bank * BANK_COLS : (bank + 1) * BANK_COLS
-                ],
+                rhs_scale=pass_planes[g][:, bank * BANK_COLS : (bank + 1) * BANK_COLS],
                 start=(g == 0),
                 stop=(g == PASSES - 1),
             )

@@ -34,7 +34,8 @@ GROUP_K = GROUP_PASSES * K_PASS
 SCALE_DMA_PASSES = (28, 4)
 LOAD_PASSES = 2
 SINGLE_PASSES = 4
-WORD_BUFS = 6
+SORT_PASSES = 4
+WORD_BUFS = 5
 X_LOADS = 2
 END_PASSES = 8
 LAST_PASSES = 2
@@ -95,24 +96,23 @@ def build_rotation_tables(nc, pool):
     return cos_sin
 
 
-def quantise_x_group(nc, flip_psum, stage, x_group, identity, codes, scales):
-    x_words = x_group.bitcast(F32)
-    pass_words = K_PASS // 2
+def quantise_x_group(nc, flip_psum, sort_pool, stage, x_group, identity, codes, scales):
+    x_words = x_group.bitcast(F32).rearrange("m (l p u) -> m l u p", p=P, u=2)
     grouped = stage.tile([P, GROUP_PASSES * P * PACK], BF16, align_bytes=256)
     grouped_words = grouped[:].bitcast(F32).rearrange("p (l m u) -> p l m u", m=P, u=2)
-    for pair in range(GROUP_PASSES // 2):
-        flipped = flip_psum.tile([P, 2, 2, P], F32)
-        for l in range(2):
-            first = (2 * pair + l) * pass_words
-            for u in range(2):
-                nc.tensor.transpose(
-                    flipped[:, l, u, :], x_words[:, first + u : first + pass_words : 2], identity[:]
-                )
-        copy = nc.vector.tensor_copy if pair % 2 == 0 else nc.scalar.copy
-        copy(
-            out=grouped_words[:, 2 * pair : 2 * pair + 2, :, :],
-            in_=flipped[:].rearrange("p l u m -> p l m u"),
-        )
+    for start in range(0, GROUP_PASSES, SORT_PASSES):
+        words = sort_pool.tile([P, SORT_PASSES, 2, P], F32)
+        nc.scalar.copy(out=words[:], in_=x_words[:, start : start + SORT_PASSES, :, :])
+        for first in range(0, SORT_PASSES, 2):
+            flipped = flip_psum.tile([P, 2, 2, P], F32)
+            for l in range(2):
+                for u in range(2):
+                    nc.tensor.transpose(flipped[:, l, u, :], words[:, first + l, u, :], identity[:])
+            copy = nc.vector.tensor_copy if first % 4 == 0 else nc.scalar.copy
+            copy(
+                out=grouped_words[:, start + first : start + first + 2, :, :],
+                in_=flipped[:].rearrange("p l u m -> p l m u"),
+            )
     nc.vector.quantize_mx(out=codes[:].bitcast(FP8X4), scales=scales[:], in_=grouped[:])
 
 
@@ -161,6 +161,7 @@ def tile_mla_pb_k_kernel(tc, x, Wq_words, Wq_scales, out):
     with ExitStack() as ctx:
         consts = ctx.enter_context(tc.tile_pool(name="consts", bufs=1))
         x_pool = ctx.enter_context(tc.tile_pool(name="x_pool", bufs=X_LOADS))
+        sort_pool = ctx.enter_context(tc.tile_pool(name="sort_pool", bufs=3))
         stage = ctx.enter_context(tc.tile_pool(name="stage", bufs=2))
         keep = ctx.enter_context(tc.tile_pool(name="keep", bufs=1))
         word_pool = ctx.enter_context(tc.tile_pool(name="word_pool", bufs=WORD_BUFS))
@@ -198,7 +199,7 @@ def tile_mla_pb_k_kernel(tc, x, Wq_words, Wq_scales, out):
         for group in range(GROUPS):
             codes = keep.tile([P, GROUP_PASSES * P], U32, name="x_codes%d" % group, align_bytes=256)
             scales = keep.tile([P, GROUP_PASSES * P], U8, name="x_scales%d" % group, align_bytes=256)
-            quantise_x_group(nc, flip_psum, stage, x_groups[group], identity, codes, scales)
+            quantise_x_group(nc, flip_psum, sort_pool, stage, x_groups[group], identity, codes, scales)
             x_codes.append(codes)
             x_scales.append(scales)
 

import math
from contextlib import ExitStack

import concourse.masks as masks
import concourse.mybir as mybir

F32 = mybir.dt.float32
BF16 = mybir.dt.bfloat16
I32 = mybir.dt.int32
U32 = mybir.dt.uint32
U8 = mybir.dt.uint8
FP8X4 = mybir.dt.float8_e4m3fn_x4
FP4X4 = mybir.dt.float4_e2m1fn_x4
ALU = mybir.AluOpType
ACT = mybir.ActivationFunctionType

B, S, E, H, DH = 2, 64, 16384, 16, 128
N = H * DH
NOPE = DH // 4
HALF = (DH - NOPE) // 2
THETA = 10000.0

P = 128
PACK = 4
K_PASS = P * PACK
PASSES = E // K_PASS
BANK_COLS = 512
BANKS = N // BANK_COLS
BANK_HEADS = BANK_COLS // DH

GROUP_PASSES = 8
GROUPS = PASSES // GROUP_PASSES
GROUP_K = GROUP_PASSES * K_PASS
SCALE_DMA_PASSES = (28, 4)
LOAD_PASSES = 2
SINGLE_PASSES = 4
SORT_PASSES = 4
WORD_BUFS = 5
X_LOADS = 2
END_PASSES = 8
LAST_PASSES = 2

TWO_PI_PARTS = (6.28125, 0.0019354820251464844, 2.0 * math.pi - 6.28125 - 0.0019354820251464844)
ROUND_MAGIC = 12582912.0

FLOPS = 2 * B * S * E * N


def build_rotation_tables(nc, pool):
    position_int = pool.tile([P, 1], I32)
    nc.gpsimd.iota(position_int[:], pattern=[[0, 1]], base=0, channel_multiplier=1)
    nc.vector.tensor_single_scalar(
        out=position_int[:], in_=position_int[:], scalar=S - 1, op=ALU.bitwise_and
    )
    position = pool.tile([P, 1], F32)
    nc.vector.tensor_copy(out=position[:], in_=position_int[:])

    ratio = THETA ** (-1.0 / HALF)
    frequency = pool.tile([P, HALF], F32)
    nc.vector.memset(frequency[:, 0:1], 1.0)
    filled = 1
    while filled < HALF:
        more = min(filled, HALF - filled)
        nc.vector.tensor_single_scalar(
            out=frequency[:, filled : filled + more],
            in_=frequency[:, 0:more],
            scalar=ratio**filled,
            op=ALU.mult,
        )
        filled += more

    angle = pool.tile([P, 2, HALF], F32)
    nc.vector.tensor_scalar(
        out=angle[:, 1, :], in0=frequency[:], scalar1=position[:, 0:1], scalar2=None, op0=ALU.mult
    )
    nc.vector.tensor_single_scalar(
        out=angle[:, 0, :], in_=angle[:, 1, :], scalar=math.pi / 2.0, op=ALU.add
    )

    turns = pool.tile([P, 2, HALF], F32)
    nc.vector.tensor_scalar(
        out=turns[:],
        in0=angle[:],
        scalar1=1.0 / (2.0 * math.pi),
        scalar2=ROUND_MAGIC,
        op0=ALU.mult,
        op1=ALU.add,
    )
    nc.vector.tensor_single_scalar(out=turns[:], in_=turns[:], scalar=ROUND_MAGIC, op=ALU.subtract)
    for part in TWO_PI_PARTS:
        nc.vector.scalar_tensor_tensor(
            out=angle[:], in0=turns[:], scalar=-part, in1=angle[:], op0=ALU.mult, op1=ALU.add
        )
    cos_sin = pool.tile([P, 2, HALF], F32)
    nc.scalar.activation(out=cos_sin[:], in_=angle[:], func=ACT.Sin)
    return cos_sin


def quantise_x_group(nc, flip_psum, sort_pool, stage, x_group, identity, codes, scales):
    x_words = x_group.bitcast(F32).rearrange("m (l p u) -> m l u p", p=P, u=2)
    grouped = stage.tile([P, GROUP_PASSES * P * PACK], BF16, align_bytes=256)
    grouped_words = grouped[:].bitcast(F32).rearrange("p (l m u) -> p l m u", m=P, u=2)
    for start in range(0, GROUP_PASSES, SORT_PASSES):
        words = sort_pool.tile([P, SORT_PASSES, 2, P], F32)
        nc.scalar.copy(out=words[:], in_=x_words[:, start : start + SORT_PASSES, :, :])
        for first in range(0, SORT_PASSES, 2):
            flipped = flip_psum.tile([P, 2, 2, P], F32)
            for l in range(2):
                for u in range(2):
                    nc.tensor.transpose(flipped[:, l, u, :], words[:, first + l, u, :], identity[:])
            copy = nc.vector.tensor_copy if first % 4 == 0 else nc.scalar.copy
            copy(
                out=grouped_words[:, start + first : start + first + 2, :, :],
                in_=flipped[:].rearrange("p l u m -> p l m u"),
            )
    nc.vector.quantize_mx(out=codes[:].bitcast(FP8X4), scales=scales[:], in_=grouped[:])


def load_scale_rows(nc, planes, Wq_scales):
    rows = Wq_scales.rearrange("g (half low) n -> low half g n", half=2)
    first = 0
    for plane, count in zip(planes, SCALE_DMA_PASSES):
        for low in range(8):
            partition = 32 * (low // 4) + low % 4
            nc.sync.dma_start(
                out=plane[partition:P:64, :, :].bitcast(I32),
                in_=rows[low, :, first : first + count, :].bitcast(I32),
            )
        first += count


def rotate_and_store(nc, out_pool, q_bank, cos_sin, out, bank):
    q = q_bank[:].rearrange("p (h d) -> p h d", d=DH)
    pairs = q[:, :, NOPE:].rearrange("p h (j e) -> p h e j", e=2)
    table_shape = [P, BANK_HEADS, 2, HALF]
    cos = cos_sin[:, 0:1, :].unsqueeze(1).to_broadcast(table_shape)
    sin = cos_sin[:, 1:2, :].unsqueeze(1).to_broadcast(table_shape)

    result = out_pool.tile([P, BANK_HEADS, DH], F32)
    by_sin = out_pool.tile([P, BANK_HEADS, 2, HALF], F32)
    first_half = result[:, :, NOPE : NOPE + HALF]
    second_half = result[:, :, NOPE + HALF :]
    nc.vector.tensor_tensor(
        out=result[:, :, NOPE:].rearrange("p h (e j) -> p h e j", e=2), in0=pairs, in1=cos, op=ALU.mult
    )
    nc.vector.tensor_tensor(out=by_sin[:], in0=pairs, in1=sin, op=ALU.mult)
    nc.scalar.copy(out=result[:, :, :NOPE], in_=q[:, :, :NOPE])
    nc.vector.tensor_tensor(out=first_half, in0=first_half, in1=by_sin[:, :, 1, :], op=ALU.subtract)
    nc.vector.tensor_tensor(out=second_half, in0=second_half, in1=by_sin[:, :, 0, :], op=ALU.add)

    heads = slice(bank * BANK_HEADS, (bank + 1) * BANK_HEADS)
    for b in range(B):
        nc.sync.dma_start(
            out=out[b, heads, :, :].rearrange("h s d -> s h d"), in_=result[b * S : (b + 1) * S, :, :]
        )


def tile_mla_pb_k_kernel(tc, x, Wq_words, Wq_scales, out):
    nc = tc.nc
    x_rows = x.rearrange("b s e -> (b s) e")
    with ExitStack() as ctx:
        consts = ctx.enter_context(tc.tile_pool(name="consts", bufs=1))
        x_pool = ctx.enter_context(tc.tile_pool(name="x_pool", bufs=X_LOADS))
        sort_pool = ctx.enter_context(tc.tile_pool(name="sort_pool", bufs=3))
        stage = ctx.enter_context(tc.tile_pool(name="stage", bufs=2))
        keep = ctx.enter_context(tc.tile_pool(name="keep", bufs=1))
        word_pool = ctx.enter_context(tc.tile_pool(name="word_pool", bufs=WORD_BUFS))
        end_pool = ctx.enter_context(tc.tile_pool(name="end_pool", bufs=1))
        out_pool = ctx.enter_context(tc.tile_pool(name="out_pool", bufs=BANKS))
        flip_psum = ctx.enter_context(tc.psum_pool(name="flip_psum", bufs=8 - BANKS))
        q_psum = ctx.enter_context(tc.psum_pool(name="q_psum", bufs=1))

        ctx.enter_context(tc.manual_schedule(engines={mybir.EngineType.SP}))

        w_planes = []
        pass_planes = []
        for count in SCALE_DMA_PASSES:
            plane = keep.tile([P, count, N], U8, name="w_planes%d" % len(w_planes), align_bytes=256)
            nc.vector.memset(plane[:].rearrange("p l n -> p (l n)").bitcast(I32), 0)
            w_planes.append(plane)
            for l in range(count):
                pass_planes.append(plane[:, l, :])

        x_groups = []
        load_k = E // X_LOADS
        for load in range(X_LOADS):
            x_part = x_pool.tile([P, load_k], BF16)
            nc.sync.dma_start(out=x_part[:], in_=x_rows[:, load * load_k : (load + 1) * load_k])
            for first in range(0, load_k, GROUP_K):
                x_groups.append(x_part[:, first : first + GROUP_K])
        load_scale_rows(nc, w_planes, Wq_scales)

        identity = consts.tile([P, P], F32)
        masks.make_identity(nc, identity[:])
        cos_sin = build_rotation_tables(nc, consts)

        x_codes = []
        x_scales = []
        for group in range(GROUPS):
            codes = keep.tile([P, GROUP_PASSES * P], U32, name="x_codes%d" % group, align_bytes=256)
            scales = keep.tile([P, GROUP_PASSES * P], U8, name="x_scales%d" % group, align_bytes=256)
            quantise_x_group(nc, flip_psum, sort_pool, stage, x_groups[group], identity, codes, scales)
            x_codes.append(codes)
            x_scales.append(scales)

        q_banks = []
        for bank in range(BANKS):
            q_bank = q_psum.tile([P, BANK_COLS], F32, name="q_bank%d" % bank)
            q_banks.append(q_bank)

        def mx_pass(g, bank, bank_words):
            group, local = divmod(g, GROUP_PASSES)
            tokens = slice(local * P, (local + 1) * P)
            nc.tensor.matmul_mx(
                out=q_banks[bank][:],
                lhsT=x_codes[group][:, tokens].bitcast(FP8X4),
                lhsT_scale=x_scales[group][:, tokens],
                rhs=bank_words.bitcast(FP4X4),
                rhs_scale=pass_planes[g][:, bank * BANK_COLS : (bank + 1) * BANK_COLS],
                start=(g == 0),
                stop=(g == PASSES - 1),
            )

        bank_bytes = 2 * BANK_COLS
        g = 0
        while g < PASSES - END_PASSES:
            passes = LOAD_PASSES if SINGLE_PASSES <= g < PASSES - END_PASSES - SINGLE_PASSES else 1
            words = word_pool.tile([P, passes, BANKS * bank_bytes], U8, align_bytes=256)
            nc.sync.dma_start(
                out=words[:].bitcast(I32), in_=Wq_words[g : g + passes].rearrange("g p c -> p g c").bitcast(I32)
            )
            for i in range(passes):
                for bank in range(BANKS):
                    mx_pass(g + i, bank, words[:, i, bank * bank_bytes : (bank + 1) * bank_bytes])
            g += passes

        first_end = PASSES - END_PASSES
        end_loads = []
        end_loads.append((0, 2, first_end, END_PASSES // 2))
        end_loads.append((0, 2, first_end + END_PASSES // 2, END_PASSES // 2))
        end_loads.append((2, 1, first_end, END_PASSES))
        end_loads.append((3, 1, first_end, END_PASSES - LAST_PASSES))
        end_loads.append((3, 1, PASSES - LAST_PASSES, LAST_PASSES))
        end_words = []
        for bank, banks, first, passes in end_loads:
            words = end_pool.tile([P, passes, banks * bank_bytes], U8, name="end_words%d" % len(end_words), align_bytes=256)
            nc.sync.dma_start(
                out=words[:].bitcast(I32),
                in_=Wq_words[first : first + passes, :, bank * bank_bytes : (bank + banks) * bank_bytes]
                .rearrange("g p c -> p g c")
                .bitcast(I32),
            )
            end_words.append(words)
        for (first_bank, banks, first, passes), words in zip(end_loads, end_words):
            for bank in range(first_bank, first_bank + banks):
                start = (bank - first_bank) * bank_bytes
                for i in range(passes):
                    mx_pass(first + i, bank, words[:, i, start : start + bank_bytes])
                if first + passes == PASSES:
                    rotate_and_store(nc, out_pool, q_banks[bank], cos_sin, out, bank)
